import numpy as np
import ml_dtypes


def mxq(x, axis, fmt="e4m3"):
    dtype, down = {"e4m3": (ml_dtypes.float8_e4m3fn, 7), "e5m2": (ml_dtypes.float8_e5m2, 14)}[fmt]
    v = np.moveaxis(np.asarray(x, np.float32).astype(ml_dtypes.bfloat16).astype(np.float64), axis, -1)
    blocks = v.reshape(v.shape[:-1] + (-1, 32))
    amax = np.abs(blocks).max(-1, keepdims=True)
    byte = np.maximum(np.where(amax > 0, np.frexp(amax)[1] - 1 + 127, 0) - down, 1)
    scale = np.exp2(byte - 127.0)
    codes = (blocks / scale).astype(np.float32).astype(dtype).astype(np.float64)
    return np.moveaxis((codes * scale).reshape(v.shape), -1, axis)


WIDE = False


def mx_kscale(k):
    if not WIDE:
        return np.ones(k)
    levels = np.array([10, -10, 5, -5, 0])
    if k % 512:
        return np.exp2(np.random.permutation(np.resize(levels, k // 32))).repeat(32)
    a = np.empty((k // 512, 16))
    for p in range(k // 512):
        a[p, :8] = np.random.permutation(np.resize(levels, 8))
        for g in range(8):
            far = levels[np.abs(levels - a[p, g]) >= 10]
            a[p, g + 8] = far[np.random.randint(len(far))]
    return np.exp2(a.ravel()).repeat(32)


BF16 = ml_dtypes.bfloat16


def bf(x):
    return np.asarray(x, np.float32).astype(BF16)


def f64(x):
    return np.asarray(x).astype(np.float64)


B, S, D = 4, 1024, 512
ROPE_BASE = 10000.0


def rope_tables():
    inv_freq = 1.0 / ROPE_BASE ** (np.arange(0, D, 2) / D)
    freqs = np.outer(np.arange(S), inv_freq)
    emb = np.concatenate([freqs, freqs], axis=-1)
    return np.cos(emb), np.sin(emb)


def rotate_half(u):
    u1, u2 = np.split(u, 2, axis=-1)
    return np.concatenate([-u2, u1], axis=-1)


def setup_inputs():
    s = mx_kscale(D)
    c, sn = rope_tables()
    w = 1.0 / np.sqrt(D)
    return {"x": bf(np.random.standard_normal((B, S, D)) * s),
            "cos": bf(c),
            "sin": bf(sn),
            "Wq": bf(np.random.standard_normal((D, D)) * w / s[None, :]),
            "Wk": bf(np.random.standard_normal((D, D)) * w / s[None, :])}


def reference(x, cos, sin, Wq, Wk):
    xq = mxq(f64(x), 2, "e4m3")
    q = xq @ mxq(f64(Wq), 1, "e4m3").T
    k = xq @ mxq(f64(Wk), 1, "e4m3").T
    c, sn = f64(cos), f64(sin)
    q_rot = q * c + rotate_half(q) * sn
    k_rot = k * c + rotate_half(k) * sn
    return q_rot, k_rot

@@ -1,0 +1,129 @@
+from contextlib import ExitStack
+
+import concourse.mybir as mybir
+from concourse.masks import make_identity
+
+F32 = mybir.dt.float32
+BF16 = mybir.dt.bfloat16
+U32 = mybir.dt.uint32
+U8 = mybir.dt.uint8
+FP8X4 = mybir.dt.float8_e4m3fn_x4
+MULT = mybir.AluOpType.mult
+ADD = mybir.AluOpType.add
+
+P = 128
+B, S, D = 4, 1024, 512
+HALF = D // 2
+T = S // P
+PAIR = 2
+N_TILES = B * T
+N_GROUPS = N_TILES // PAIR
+AHEAD = 3
+LOAD_T = 4
+
+FLOPS = 2 * B * S * D * (2 * D)
+
+
+def tile_attention_pa_t_kernel(tc, x, cos, sin, Wq, Wk, out_0, out_1):
+    nc = tc.nc
+    with ExitStack() as ctx:
+        ctx.enter_context(tc.manual_schedule())
+        keep = ctx.enter_context(tc.tile_pool(name="keep", bufs=1))
+        stage = ctx.enter_context(tc.tile_pool(name="stage", bufs=3))
+        results = ctx.enter_context(tc.tile_pool(name="results", bufs=8))
+        psum_t = ctx.enter_context(tc.psum_pool(name="psum_t", bufs=2))
+        psum_o = ctx.enter_context(tc.psum_pool(name="psum_o", bufs=6))
+
+        w_sb = keep.tile([P, 2, D // P, D], BF16)
+        x_sb = keep.tile([P, B, T, D], BF16)
+        cos_sb = keep.tile([P, T, D], BF16)
+        sin_swapped = keep.tile([P, T, 2, HALF], BF16)
+        by_partition = "(p t) d -> p t d"
+        for m, w in enumerate((Wq, Wk)):
+            nc.sync.dma_start(out=w_sb[:, m], in_=w.rearrange("(c p) k -> p c k", p=P))
+        for b in range(B):
+            for t0 in range(0, T, LOAD_T):
+                ts = slice(t0, t0 + LOAD_T)
+                nc.sync.dma_start(out=x_sb[:, b, ts, :], in_=x[b].rearrange(by_partition, t=T)[:, ts, :])
+            if b == 0:
+                nc.sync.dma_start(out=cos_sb[:], in_=cos.rearrange(by_partition, t=T))
+                for h in range(2):
+                    nc.sync.dma_start(
+                        out=sin_swapped[:, :, 1 - h, :],
+                        in_=sin.rearrange(by_partition, t=T)[:, :, h * HALF : (h + 1) * HALF],
+                    )
+
+        ident = keep.tile([P, P], F32)
+        make_identity(nc, ident[:])
+
+        def quantise_rows(row_tiles, codes, scales):
+            bank = psum_t.tile([P, PAIR, 2, P], F32)
+            for i, rows in enumerate(row_tiles):
+                words = rows.bitcast(F32)
+                for u in range(2):
+                    nc.tensor.transpose(bank[:, i, u, :], words[:, u : 2 * P : 2], ident[:])
+            grouped = stage.tile([P, PAIR * P * 4], BF16, align_bytes=64)
+            nc.scalar.copy(
+                out=grouped[:].bitcast(F32).rearrange("p (i r u) -> p i r u", i=PAIR, u=2),
+                in_=bank[:].rearrange("p i u r -> p i r u"),
+            )
+            nc.vector.quantize_mx(out=codes.bitcast(FP8X4), scales=scales, in_=grouped[:])
+
+        w_codes = keep.tile([P, 2 * D], U32, align_bytes=64)
+        w_scales = keep.tile([P, 2 * D], U8, align_bytes=64)
+        for m in range(2):
+            for c in range(0, D // P, PAIR):
+                cols = slice(m * D + c * P, m * D + (c + PAIR) * P)
+                quantise_rows([w_sb[:, m, c + i, :] for i in range(PAIR)], w_codes[:, cols], w_scales[:, cols])
+
+        x_codes = keep.tile([P, N_TILES * P], U32, align_bytes=64)
+        x_scales = keep.tile([P, N_TILES * P], U8, align_bytes=64)
+
+        def prepare(g):
+            cols = slice(g * PAIR * P, (g + 1) * PAIR * P)
+            tiles = [divmod(g * PAIR + i, T) for i in range(PAIR)]
+            quantise_rows([x_sb[:, b, t, :] for b, t in tiles], x_codes[:, cols], x_scales[:, cols])
+
+        def project(g):
+            for i in range(PAIR):
+                n = g * PAIR + i
+                b, t = divmod(n, T)
+                straight = results.tile([P, 2, 2, HALF], F32)
+                crossed = results.tile([P, 2, 2, HALF], F32)
+                for m in range(2):
+                    acc = psum_o.tile([P, D], F32)
+                    nc.tensor.matmul_mx(
+                        out=acc[:],
+                        lhsT=x_codes[:, n * P : (n + 1) * P].bitcast(FP8X4),
+                        lhsT_scale=x_scales[:, n * P : (n + 1) * P],
+                        rhs=w_codes[:, m * D : (m + 1) * D].bitcast(FP8X4),
+                        rhs_scale=w_scales[:, m * D : (m + 1) * D],
+                        start=True,
+                        stop=True,
+                    )
+                    nc.vector.tensor_tensor(
+                        out=straight[:, m].rearrange("p h j -> p (h j)"), in0=acc[:], in1=cos_sb[:, t, :], op=MULT
+                    )
+                    nc.vector.tensor_tensor(
+                        out=crossed[:, m].rearrange("p h j -> p (h j)"),
+                        in0=acc[:],
+                        in1=sin_swapped[:, t].rearrange("p h j -> p (h j)"),
+                        op=MULT,
+                    )
+                for h in range(2):
+                    nc.gpsimd.tensor_tensor(
+                        out=straight[:, :, h, :], in0=straight[:, :, h, :], in1=crossed[:, :, 1 - h, :], op=ADD
+                    )
+                for m, out in enumerate((out_0, out_1)):
+                    nc.sync.dma_start(
+                        out=out[b].rearrange(by_partition, t=T)[:, t, :],
+                        in_=straight[:, m].rearrange("p h j -> p (h j)"),
+                    )
+
+        for g in range(AHEAD):
+            prepare(g)
+        nc.vector.tensor_scalar_mul(out=sin_swapped[:, :, 1, :], in0=sin_swapped[:, :, 1, :], scalar1=-1.0)
+        for g in range(N_GROUPS):
+            project(g)
+            if g + AHEAD < N_GROUPS:
+                prepare(g + AHEAD)

@@ -15,115 +15,296 @@ P = 128
 B, S, D = 4, 1024, 512
 HALF = D // 2
 T = S // P
-PAIR = 2
-N_TILES = B * T
-N_GROUPS = N_TILES // PAIR
-AHEAD = 3
-LOAD_T = 4
+F = D // P
+
+KINDS = "TTDTDTTDTDTTDTTD"
+T_POSITIONS = (0, 2, 4, 6, 7)
+D_POSITIONS = (1, 3, 5)
+LAG = 2
+N_GPSIMD = {i: 3 for i in range(16)}
+CHUNKS = 2
 
 FLOPS = 2 * B * S * D * (2 * D)
 
 
 def tile_attention_pa_t_kernel(tc, x, cos, sin, Wq, Wk, out_0, out_1):
     nc = tc.nc
+    outs = [o.rearrange("b (p t) d -> p b t d", t=T) for o in (out_0, out_1)]
     with ExitStack() as ctx:
         ctx.enter_context(tc.manual_schedule())
         keep = ctx.enter_context(tc.tile_pool(name="keep", bufs=1))
-        stage = ctx.enter_context(tc.tile_pool(name="stage", bufs=3))
-        results = ctx.enter_context(tc.tile_pool(name="results", bufs=8))
-        psum_t = ctx.enter_context(tc.psum_pool(name="psum_t", bufs=2))
-        psum_o = ctx.enter_context(tc.psum_pool(name="psum_o", bufs=6))
+        work = ctx.enter_context(tc.tile_pool(name="work", bufs=2))
+        psum_acc = ctx.enter_context(tc.psum_pool(name="psum_acc", bufs=4))
+        psum_tr = ctx.enter_context(tc.psum_pool(name="psum_tr", bufs=4))
 
-        w_sb = keep.tile([P, 2, D // P, D], BF16)
-        x_sb = keep.tile([P, B, T, D], BF16)
-        cos_sb = keep.tile([P, T, D], BF16)
-        sin_swapped = keep.tile([P, T, 2, HALF], BF16)
-        by_partition = "(p t) d -> p t d"
-        for m, w in enumerate((Wq, Wk)):
-            nc.sync.dma_start(out=w_sb[:, m], in_=w.rearrange("(c p) k -> p c k", p=P))
-        for b in range(B):
-            for t0 in range(0, T, LOAD_T):
-                ts = slice(t0, t0 + LOAD_T)
-                nc.sync.dma_start(out=x_sb[:, b, ts, :], in_=x[b].rearrange(by_partition, t=T)[:, ts, :])
-            if b == 0:
-                nc.sync.dma_start(out=cos_sb[:], in_=cos.rearrange(by_partition, t=T))
-                for h in range(2):
-                    nc.sync.dma_start(
-                        out=sin_swapped[:, :, 1 - h, :],
-                        in_=sin.rearrange(by_partition, t=T)[:, :, h * HALF : (h + 1) * HALF],
-                    )
+        x_view = x.rearrange("b (p t) d -> p b t d", t=T)
+        cos_view = cos.rearrange("(p t) d -> p t d", t=T)
+        sin_view = sin.rearrange("(p t) d -> p t d", t=T)
+        w_rows, x_rows, table_rows = {}, {}, {}
+
+        def load_w(m):
+            w_sb = keep.tile([P, F, D], BF16, name="w_sb%d" % m)
+            nc.sync.dma_start(out=w_sb[:], in_=(Wq, Wk)[m].rearrange("(c p) k -> p c k", p=P))
+            w_rows[m] = w_sb
+
+        def load_x(t0, t1):
+            x_sb = keep.tile([P, B, t1 - t0, D], BF16, name="x_sb%d" % t0)
+            step = B if t1 - t0 == 1 else 2
+            for b in range(0, B, step):
+                nc.sync.dma_start(out=x_sb[:, b : b + step], in_=x_view[:, b : b + step, t0:t1, :])
+            for t in range(t0, t1):
+                x_rows[t] = [x_sb[:, b, t - t0, :] for b in range(B)]
+
+        def load_tables(t0, t1):
+            cos_sb = keep.tile([P, t1 - t0, D], BF16, name="cos_sb%d" % t0)
+            sin_sb = keep.tile([P, t1 - t0, D], BF16, name="sin_sb%d" % t0)
+            nc.sync.dma_start(out=cos_sb[:], in_=cos_view[:, t0:t1, :])
+            nc.sync.dma_start(out=sin_sb[:], in_=sin_view[:, t0:t1, :])
+            for t in range(t0, t1):
+                table_rows[t] = (cos_sb[:, t - t0, :], sin_sb[:, t - t0, :])
+
+        load_w(0)
+        load_x(0, 1)
+        load_tables(0, 1)
+        load_w(1)
+        load_x(1, 2)
+        load_tables(1, 2)
+        load_x(2, 4)
+        load_tables(2, 4)
+        load_x(4, 6)
+        load_tables(4, 8)
+        load_x(6, 8)
 
         ident = keep.tile([P, P], F32)
         make_identity(nc, ident[:])
+        ident_b = keep.tile([P, P], BF16)
+        make_identity(nc, ident_b[:])
 
-        def quantise_rows(row_tiles, codes, scales):
-            bank = psum_t.tile([P, PAIR, 2, P], F32)
-            for i, rows in enumerate(row_tiles):
+        def negate_sin(t):
+            first = table_rows[t][1][:, 0:HALF]
+            nc.vector.tensor_scalar_mul(out=first, in0=first, scalar1=-1.0)
+
+        def turn(rows_list, grouped):
+            bank = psum_tr.tile([P, 2, 2, P], F32, tag="tr")
+            for j, rows in enumerate(rows_list):
                 words = rows.bitcast(F32)
                 for u in range(2):
-                    nc.tensor.transpose(bank[:, i, u, :], words[:, u : 2 * P : 2], ident[:])
-            grouped = stage.tile([P, PAIR * P * 4], BF16, align_bytes=64)
+                    nc.tensor.transpose(bank[:, j, u, :], words[:, u : 2 * P : 2], ident[:])
             nc.scalar.copy(
-                out=grouped[:].bitcast(F32).rearrange("p (i r u) -> p i r u", i=PAIR, u=2),
+                out=grouped.bitcast(F32).rearrange("p (i r u) -> p i r u", i=2, u=2),
                 in_=bank[:].rearrange("p i u r -> p i r u"),
             )
-            nc.vector.quantize_mx(out=codes.bitcast(FP8X4), scales=scales, in_=grouped[:])
 
         w_codes = keep.tile([P, 2 * D], U32, align_bytes=64)
         w_scales = keep.tile([P, 2 * D], U8, align_bytes=64)
-        for m in range(2):
-            for c in range(0, D // P, PAIR):
-                cols = slice(m * D + c * P, m * D + (c + PAIR) * P)
-                quantise_rows([w_sb[:, m, c + i, :] for i in range(PAIR)], w_codes[:, cols], w_scales[:, cols])
+        x_codes = keep.tile([P, T * B * P], U32, align_bytes=64)
+        x_scales = keep.tile([P, T * B * P], U8, align_bytes=64)
 
-        x_codes = keep.tile([P, N_TILES * P], U32, align_bytes=64)
-        x_scales = keep.tile([P, N_TILES * P], U8, align_bytes=64)
+        def prepare_w(m):
+            for c in range(0, F, 2):
+                cols = slice(m * D + c * P, m * D + (c + 2) * P)
+                w_grouped = work.tile([P, 2 * P * 4], BF16, align_bytes=64, tag="w_grouped")
+                turn([w_rows[m][:, c + i, :] for i in range(2)], w_grouped[:])
+                nc.vector.quantize_mx(out=w_codes[:, cols].bitcast(FP8X4), scales=w_scales[:, cols], in_=w_grouped[:])
 
-        def prepare(g):
-            cols = slice(g * PAIR * P, (g + 1) * PAIR * P)
-            tiles = [divmod(g * PAIR + i, T) for i in range(PAIR)]
-            quantise_rows([x_sb[:, b, t, :] for b, t in tiles], x_codes[:, cols], x_scales[:, cols])
+        x_grouped = {}
 
-        def project(g):
-            for i in range(PAIR):
-                n = g * PAIR + i
-                b, t = divmod(n, T)
-                straight = results.tile([P, 2, 2, HALF], F32)
-                crossed = results.tile([P, 2, 2, HALF], F32)
-                for m in range(2):
-                    acc = psum_o.tile([P, D], F32)
-                    nc.tensor.matmul_mx(
-                        out=acc[:],
-                        lhsT=x_codes[:, n * P : (n + 1) * P].bitcast(FP8X4),
-                        lhsT_scale=x_scales[:, n * P : (n + 1) * P],
-                        rhs=w_codes[:, m * D : (m + 1) * D].bitcast(FP8X4),
-                        rhs_scale=w_scales[:, m * D : (m + 1) * D],
-                        start=True,
-                        stop=True,
-                    )
-                    nc.vector.tensor_tensor(
-                        out=straight[:, m].rearrange("p h j -> p (h j)"), in0=acc[:], in1=cos_sb[:, t, :], op=MULT
-                    )
-                    nc.vector.tensor_tensor(
-                        out=crossed[:, m].rearrange("p h j -> p (h j)"),
-                        in0=acc[:],
-                        in1=sin_swapped[:, t].rearrange("p h j -> p (h j)"),
-                        op=MULT,
-                    )
-                for h in range(2):
-                    nc.gpsimd.tensor_tensor(
-                        out=straight[:, :, h, :], in0=straight[:, :, h, :], in1=crossed[:, :, 1 - h, :], op=ADD
-                    )
-                for m, out in enumerate((out_0, out_1)):
-                    nc.sync.dma_start(
-                        out=out[b].rearrange(by_partition, t=T)[:, t, :],
-                        in_=straight[:, m].rearrange("p h j -> p (h j)"),
-                    )
+        def turn_x(t, half):
+            if half == 0:
+                x_grouped[t] = work.tile([P, B * P * 4], BF16, align_bytes=64, tag="x_grouped", bufs=3, name="x_grouped")
+            cols = slice(half * 2 * P * 4, (half + 1) * 2 * P * 4)
+            turn(x_rows[t][2 * half : 2 * half + 2], x_grouped[t][:, cols])
 
-        for g in range(AHEAD):
-            prepare(g)
-        nc.vector.tensor_scalar_mul(out=sin_swapped[:, :, 1, :], in0=sin_swapped[:, :, 1, :], scalar1=-1.0)
-        for g in range(N_GROUPS):
-            project(g)
-            if g + AHEAD < N_GROUPS:
-                prepare(g + AHEAD)
+        def quantise_x(t):
+            cols = slice(t * B * P, (t + 1) * B * P)
+            nc.vector.quantize_mx(out=x_codes[:, cols].bitcast(FP8X4), scales=x_scales[:, cols], in_=x_grouped[t][:])
+
+        tables = {}
+
+        def turn_tables(t):
+            bank = psum_tr.tile([P, 2, F, P], BF16, tag="tr")
+            for k, table in enumerate(table_rows[t]):
+                for f in range(F):
+                    source = f if k == 0 else (f + F // 2) % F
+                    nc.tensor.transpose(bank[:, k, f, :], table[:, source * P : (source + 1) * P], ident_b[:])
+            turned = keep.tile([P, 2, F, P], BF16, name="turned%d" % t)
+            nc.scalar.copy(out=turned[:], in_=bank[:])
+            tables[t] = turned
+
+        def project(lhs, lhs_scale, rhs, rhs_scale):
+            acc = psum_acc.tile([P, D], F32, tag="acc")
+            nc.tensor.matmul_mx(
+                out=acc[:],
+                lhsT=lhs.bitcast(FP8X4),
+                lhsT_scale=lhs_scale,
+                rhs=rhs.bitcast(FP8X4),
+                rhs_scale=rhs_scale,
+                start=True,
+                stop=True,
+            )
+            return acc
+
+        def t_matmuls(t, m, half):
+            accs = []
+            tokens = slice(t * B * P, (t + 1) * B * P)
+            for f in range(2 * half, 2 * half + 2):
+                feats = slice(m * D + f * P, m * D + (f + 1) * P)
+                accs.append(project(w_codes[:, feats], w_scales[:, feats], x_codes[:, tokens], x_scales[:, tokens]))
+            return accs
+
+        def t_products(t, half, accs, straight, crossed, n_gpsimd):
+            by_batch = "p (b s) -> p b s"
+            n_here = min(max(n_gpsimd - 2 * half, 0), 2)
+            if n_here:
+                copied = work.tile([P, 2, B * P], F32, tag="t_copied", bufs=3)
+            for i, acc in enumerate(accs):
+                f = 2 * half + i
+                if i < n_here and i == 1:
+                    nc.scalar.copy(out=copied[:, i, :], in_=acc[:])
+                for k, dest in enumerate((straight, crossed)):
+                    if k == 0 or i >= n_here:
+                        nc.vector.tensor_tensor(
+                            out=dest[:, f, :].rearrange(by_batch, b=B),
+                            in0=acc[:].rearrange(by_batch, b=B),
+                            in1=tables[t][:, k, f, :].unsqueeze(1).to_broadcast([P, B, P]),
+                            op=MULT,
+                        )
+                if i < n_here and i == 0:
+                    nc.scalar.copy(out=copied[:, i, :], in_=acc[:])
+            if n_here:
+                mine = slice(2 * half, 2 * half + n_here)
+                nc.gpsimd.tensor_tensor(
+                    out=crossed[:, mine, :].rearrange("p f (b s) -> p f b s", b=B),
+                    in0=copied[:, 0:n_here, :].rearrange("p f (b s) -> p f b s", b=B),
+                    in1=tables[t][:, 1, mine, :].unsqueeze(2).to_broadcast([P, n_here, B, P]),
+                    op=MULT,
+                )
+
+        def t_sums(t, m, b, straight, crossed, summed):
+            bank = psum_tr.tile([P, D], F32, tag="tr")
+            tokens = slice(b * P, (b + 1) * P)
+            for f in range(F):
+                feats = slice(f * P, (f + 1) * P)
+                nc.tensor.matmul(
+                    bank[:, feats], lhsT=straight[:, f, tokens], rhs=ident[:], is_transpose=True, start=True, stop=False
+                )
+                nc.tensor.matmul(
+                    bank[:, feats],
+                    lhsT=crossed[:, (f + F // 2) % F, tokens],
+                    rhs=ident[:],
+                    is_transpose=True,
+                    start=False,
+                    stop=True,
+                )
+            nc.scalar.copy(out=summed[:, b, :], in_=bank[:])
+            if b % 2 == 1:
+                nc.sync.dma_start(out=outs[m][:, b - 1 : b + 1, t, :], in_=summed[:, b - 1 : b + 1, :])
+
+        def d_matmuls(t, half, i):
+            n = t * B + 2 * half + i
+            tokens = slice(n * P, (n + 1) * P)
+            accs = []
+            for m in range(2):
+                feats = slice(m * D, (m + 1) * D)
+                accs.append(project(x_codes[:, tokens], x_scales[:, tokens], w_codes[:, feats], w_scales[:, feats]))
+            return accs
+
+        def d_products(t, half, i, accs):
+            straight = work.tile([P, 2, D], F32, tag="d_straight", bufs=4)
+            crossed = work.tile([P, 2, D], F32, tag="d_crossed", bufs=3)
+            by_half = "p (h j) -> p h j"
+            for m, acc in enumerate(accs):
+                nc.vector.tensor_tensor(out=straight[:, m, :], in0=acc[:], in1=table_rows[t][0], op=MULT)
+                nc.vector.tensor_tensor(
+                    out=crossed[:, m, :].rearrange(by_half, h=2),
+                    in0=acc[:].rearrange(by_half, h=2)[:, ::-1, :],
+                    in1=table_rows[t][1].rearrange(by_half, h=2),
+                    op=MULT,
+                )
+            nc.gpsimd.tensor_tensor(out=straight[:], in0=straight[:], in1=crossed[:], op=ADD)
+            for m in range(2):
+                nc.sync.dma_start(out=outs[m][:, 2 * half + i, t, :], in_=straight[:, m, :])
+
+        queues = {
+            "T": [(t, m) for t in T_POSITIONS for m in range(2)],
+            "D": [(t, half) for t in D_POSITIONS for half in range(2)],
+        }
+        taken = {"T": 0, "D": 0}
+        groups = []
+        first_use = {}
+        for i, kind in enumerate(KINDS):
+            t, part = queues[kind][taken[kind]]
+            taken[kind] += 1
+            first_use.setdefault(t, len(groups))
+            for half in range(2):
+                groups.append((kind, i, t, part, half))
+
+        prepare = []
+        for t in sorted(first_use, key=first_use.get):
+            due = first_use[t] - 3
+            prepare += [(due, t, turn_x, (t, 0)), (due, t, turn_x, (t, 1))]
+            if t in T_POSITIONS:
+                prepare.append((due, t, turn_tables, (t,)))
+        left = {t: 3 if t in T_POSITIONS else 2 for t in first_use}
+        sums = []
+        state = {"prepared": 0, "summed": 0}
+        to_quantise = []
+
+        def next_prepare():
+            due, t, call, arguments = prepare[state["prepared"]]
+            state["prepared"] += 1
+            call(*arguments)
+            left[t] -= 1
+            if call == turn_x and arguments[1] == 1:
+                to_quantise.append(t)
+            if call == turn_x and arguments[1] == 0:
+                negate_sin(t)
+
+        def next_sum():
+            call_arguments = sums[state["summed"]][1]
+            state["summed"] += 1
+            t_sums(*call_arguments)
+
+        def matmuls(g):
+            kind, i, t, part, half = groups[g]
+            return t_matmuls(t, part, half) if kind == "T" else d_matmuls(t, part, half)
+
+        prepare_w(0)
+        next_prepare()
+        next_prepare()
+        for t in to_quantise:
+            quantise_x(t)
+        to_quantise.clear()
+        next_prepare()
+        accs = matmuls(0)
+        results = {}
+        for g, (kind, i, t, part, half) in enumerate(groups):
+            if g == 1:
+                prepare_w(1)
+            following = matmuls(g + 1) if g + 1 < len(groups) else []
+            if kind == "T":
+                if half == 0:
+                    straight = work.tile([P, F, B * P], F32, tag="t_straight", bufs=3)
+                    crossed = work.tile([P, F, B * P], F32, tag="t_crossed", bufs=3)
+                    results[i] = (straight, crossed)
+                straight, crossed = results[i]
+                t_products(t, half, accs, straight, crossed, N_GPSIMD.get(i, 4))
+                if half == 1:
+                    summed = work.tile([P, B, D], F32, tag="t_summed", bufs=2)
+                    for b in range(B):
+                        sums.append((g + LAG, (t, part, b, straight, crossed, summed)))
+            else:
+                d_products(t, part, half, accs)
+            accs = following
+            for t in to_quantise:
+                quantise_x(t)
+            to_quantise.clear()
+            count = 0
+            while state["prepared"] < len(prepare) and (count == 0 or prepare[state["prepared"]][0] <= g) and (prepare[state["prepared"]][0] <= g + 4):
+                next_prepare()
+                count += 1
+            while count < CHUNKS and state["summed"] < len(sums) and sums[state["summed"]][0] <= g:
+                next_sum()
+                count += 1
+        while state["summed"] < len(sums):
+            next_sum()

@@ -17,12 +17,13 @@ HALF = D // 2
 T = S // P
 F = D // P
 
-KINDS = "TTDTDTTDTDTTDTTD"
+KINDS = "TTTTDTDTDTTDTDTDTTDTDTDTTDTDTDTT"
 T_POSITIONS = (0, 2, 4, 6, 7)
 D_POSITIONS = (1, 3, 5)
-LAG = 2
-N_GPSIMD = {i: 3 for i in range(16)}
-CHUNKS = 2
+LAG = 3
+GPSIMD_BLOCKS = (2, 2, 2, 2, 1, 2, 1, 1, 2, 1, 1, 2, 1, 1, 2, 1, 1, 1, 0, 0)
+CHUNKS = {"T": 2, "D": 2}
+AHEAD = 4
 
 FLOPS = 2 * B * S * D * (2 * D)
 
@@ -42,18 +43,19 @@ def tile_attention_pa_t_kernel(tc, x, cos, sin, Wq, Wk, out_0, out_1):
         sin_view = sin.rearrange("(p t) d -> p t d", t=T)
         w_rows, x_rows, table_rows = {}, {}, {}
 
-        def load_w(m):
-            w_sb = keep.tile([P, F, D], BF16, name="w_sb%d" % m)
-            nc.sync.dma_start(out=w_sb[:], in_=(Wq, Wk)[m].rearrange("(c p) k -> p c k", p=P))
-            w_rows[m] = w_sb
+        def load_w(m, pair):
+            w_sb = keep.tile([P, 2, D], BF16, name="w_sb%d%d" % (m, pair))
+            nc.sync.dma_start(out=w_sb[:], in_=(Wq, Wk)[m].rearrange("(h c p) k -> p h c k", h=2, p=P)[:, :, pair, :])
+            for h in range(2):
+                w_rows[m, pair + 2 * h] = w_sb[:, h, :]
 
         def load_x(t0, t1):
-            x_sb = keep.tile([P, B, t1 - t0, D], BF16, name="x_sb%d" % t0)
-            step = B if t1 - t0 == 1 else 2
-            for b in range(0, B, step):
-                nc.sync.dma_start(out=x_sb[:, b : b + step], in_=x_view[:, b : b + step, t0:t1, :])
-            for t in range(t0, t1):
-                x_rows[t] = [x_sb[:, b, t - t0, :] for b in range(B)]
+            for b in range(0, B, 2):
+                x_sb = keep.tile([P, 2, t1 - t0, D], BF16, name="x_sb%d%d" % (t0, b))
+                nc.sync.dma_start(out=x_sb[:], in_=x_view[:, b : b + 2, t0:t1, :])
+                for t in range(t0, t1):
+                    for i in range(2):
+                        x_rows[t, b + i] = x_sb[:, i, t - t0, :]
 
         def load_tables(t0, t1):
             cos_sb = keep.tile([P, t1 - t0, D], BF16, name="cos_sb%d" % t0)
@@ -63,11 +65,13 @@ def tile_attention_pa_t_kernel(tc, x, cos, sin, Wq, Wk, out_0, out_1):
             for t in range(t0, t1):
                 table_rows[t] = (cos_sb[:, t - t0, :], sin_sb[:, t - t0, :])
 
-        load_w(0)
+        load_w(0, 0)
         load_x(0, 1)
         load_tables(0, 1)
-        load_w(1)
+        load_w(0, 1)
         load_x(1, 2)
+        load_w(1, 0)
+        load_w(1, 1)
         load_tables(1, 2)
         load_x(2, 4)
         load_tables(2, 4)
@@ -84,13 +88,13 @@ def tile_attention_pa_t_kernel(tc, x, cos, sin, Wq, Wk, out_0, out_1):
             first = table_rows[t][1][:, 0:HALF]
             nc.vector.tensor_scalar_mul(out=first, in0=first, scalar1=-1.0)
 
-        def turn(rows_list, grouped):
+        def turn(rows_list, grouped, copy):
             bank = psum_tr.tile([P, 2, 2, P], F32, tag="tr")
             for j, rows in enumerate(rows_list):
                 words = rows.bitcast(F32)
                 for u in range(2):
                     nc.tensor.transpose(bank[:, j, u, :], words[:, u : 2 * P : 2], ident[:])
-            nc.scalar.copy(
+            copy(
                 out=grouped.bitcast(F32).rearrange("p (i r u) -> p i r u", i=2, u=2),
                 in_=bank[:].rearrange("p i u r -> p i r u"),
             )
@@ -100,20 +104,29 @@ def tile_attention_pa_t_kernel(tc, x, cos, sin, Wq, Wk, out_0, out_1):
         x_codes = keep.tile([P, T * B * P], U32, align_bytes=64)
         x_scales = keep.tile([P, T * B * P], U8, align_bytes=64)
 
-        def prepare_w(m):
-            for c in range(0, F, 2):
-                cols = slice(m * D + c * P, m * D + (c + 2) * P)
-                w_grouped = work.tile([P, 2 * P * 4], BF16, align_bytes=64, tag="w_grouped")
-                turn([w_rows[m][:, c + i, :] for i in range(2)], w_grouped[:])
-                nc.vector.quantize_mx(out=w_codes[:, cols].bitcast(FP8X4), scales=w_scales[:, cols], in_=w_grouped[:])
+        w_grouped = {}
+
+        def turn_w(m, pair, copy):
+            w_grouped[m, pair] = work.tile([P, 2 * P * 4], BF16, align_bytes=64, tag="w_grouped", bufs=3, name="w_grouped")
+            turn([w_rows[m, pair], w_rows[m, pair + 2]], w_grouped[m, pair][:], copy)
+
+        def quantise_w(m, pair):
+            for h in range(2):
+                block = m * D + (pair + 2 * h) * P
+                cols = slice(block, block + P)
+                nc.vector.quantize_mx(
+                    out=w_codes[:, cols].bitcast(FP8X4),
+                    scales=w_scales[:, cols],
+                    in_=w_grouped[m, pair][:, h * P * 4 : (h + 1) * P * 4],
+                )
 
         x_grouped = {}
 
-        def turn_x(t, half):
+        def turn_x(t, half, copy):
             if half == 0:
                 x_grouped[t] = work.tile([P, B * P * 4], BF16, align_bytes=64, tag="x_grouped", bufs=3, name="x_grouped")
             cols = slice(half * 2 * P * 4, (half + 1) * 2 * P * 4)
-            turn(x_rows[t][2 * half : 2 * half + 2], x_grouped[t][:, cols])
+            turn([x_rows[t, 2 * half], x_rows[t, 2 * half + 1]], x_grouped[t][:, cols], copy)
 
         def quantise_x(t):
             cols = slice(t * B * P, (t + 1) * B * P)
@@ -129,7 +142,7 @@ def tile_attention_pa_t_kernel(tc, x, cos, sin, Wq, Wk, out_0, out_1):
                     nc.tensor.transpose(bank[:, k, f, :], table[:, source * P : (source + 1) * P], ident_b[:])
             turned = keep.tile([P, 2, F, P], BF16, name="turned%d" % t)
             nc.scalar.copy(out=turned[:], in_=bank[:])
-            tables[t] = turned
+            tables[t] = turned[:].rearrange("p k (h c) s -> p k h c s", h=2)
 
         def project(lhs, lhs_scale, rhs, rhs_scale):
             acc = psum_acc.tile([P, D], F32, tag="acc")
@@ -144,64 +157,62 @@ def tile_attention_pa_t_kernel(tc, x, cos, sin, Wq, Wk, out_0, out_1):
             )
             return acc
 
-        def t_matmuls(t, m, half):
+        def t_matmuls(t, m, pair):
             accs = []
             tokens = slice(t * B * P, (t + 1) * B * P)
-            for f in range(2 * half, 2 * half + 2):
-                feats = slice(m * D + f * P, m * D + (f + 1) * P)
+            for h in range(2):
+                block = m * D + (pair + 2 * h) * P
+                feats = slice(block, block + P)
                 accs.append(project(w_codes[:, feats], w_scales[:, feats], x_codes[:, tokens], x_scales[:, tokens]))
             return accs
 
-        def t_products(t, half, accs, straight, crossed, n_gpsimd):
+        def t_products(t, pair, accs, n_gpsimd):
+            straight = work.tile([P, 2, B * P], F32, tag="t_straight", bufs=5)
+            crossed = work.tile([P, 2, B * P], F32, tag="t_crossed", bufs=5)
             by_batch = "p (b s) -> p b s"
-            n_here = min(max(n_gpsimd - 2 * half, 0), 2)
-            if n_here:
-                copied = work.tile([P, 2, B * P], F32, tag="t_copied", bufs=3)
-            for i, acc in enumerate(accs):
-                f = 2 * half + i
-                if i < n_here and i == 1:
-                    nc.scalar.copy(out=copied[:, i, :], in_=acc[:])
+            if n_gpsimd:
+                copied = work.tile([P, 2, B * P], F32, tag="t_copied", bufs=4)
+            for h, acc in enumerate(accs):
+                mine = h < n_gpsimd
                 for k, dest in enumerate((straight, crossed)):
-                    if k == 0 or i >= n_here:
+                    if k == 0 or not mine:
                         nc.vector.tensor_tensor(
-                            out=dest[:, f, :].rearrange(by_batch, b=B),
+                            out=dest[:, h, :].rearrange(by_batch, b=B),
                             in0=acc[:].rearrange(by_batch, b=B),
-                            in1=tables[t][:, k, f, :].unsqueeze(1).to_broadcast([P, B, P]),
+                            in1=tables[t][:, k, h, pair, :].unsqueeze(1).to_broadcast([P, B, P]),
                             op=MULT,
                         )
-                if i < n_here and i == 0:
-                    nc.scalar.copy(out=copied[:, i, :], in_=acc[:])
-            if n_here:
-                mine = slice(2 * half, 2 * half + n_here)
+                if mine:
+                    nc.scalar.copy(out=copied[:, h, :], in_=acc[:])
+            if n_gpsimd:
+                by_batch = "p h (b s) -> p h b s"
                 nc.gpsimd.tensor_tensor(
-                    out=crossed[:, mine, :].rearrange("p f (b s) -> p f b s", b=B),
-                    in0=copied[:, 0:n_here, :].rearrange("p f (b s) -> p f b s", b=B),
-                    in1=tables[t][:, 1, mine, :].unsqueeze(2).to_broadcast([P, n_here, B, P]),
+                    out=crossed[:, 0:n_gpsimd, :].rearrange(by_batch, b=B),
+                    in0=copied[:, 0:n_gpsimd, :].rearrange(by_batch, b=B),
+                    in1=tables[t][:, 1, 0:n_gpsimd, pair, :].unsqueeze(2).to_broadcast([P, n_gpsimd, B, P]),
                     op=MULT,
                 )
+            return straight, crossed
 
-        def t_sums(t, m, b, straight, crossed, summed):
-            bank = psum_tr.tile([P, D], F32, tag="tr")
-            tokens = slice(b * P, (b + 1) * P)
-            for f in range(F):
-                feats = slice(f * P, (f + 1) * P)
-                nc.tensor.matmul(
-                    bank[:, feats], lhsT=straight[:, f, tokens], rhs=ident[:], is_transpose=True, start=True, stop=False
+        def t_sums(t, m, pair, b, straight, crossed, summed):
+            bank = psum_tr.tile([P, 2, 2, P], F32, tag="tr")
+            for i in range(2):
+                tokens = slice((b + i) * P, (b + i + 1) * P)
+                for h in range(2):
+                    nc.tensor.matmul(
+                        bank[:, i, h, :], lhsT=straight[:, h, tokens], rhs=ident[:], is_transpose=True, start=True, stop=False
+                    )
+                    nc.tensor.matmul(
+                        bank[:, i, h, :], lhsT=crossed[:, 1 - h, tokens], rhs=ident[:], is_transpose=True, start=False, stop=True
+                    )
+            nc.scalar.copy(out=summed[:, b : b + 2, :, pair, :], in_=bank[:])
+            if pair == 1:
+                nc.sync.dma_start(
+                    out=outs[m][:, b : b + 2, t, :], in_=summed[:, b : b + 2].rearrange("p b h c j -> p b (h c j)")
                 )
-                nc.tensor.matmul(
-                    bank[:, feats],
-                    lhsT=crossed[:, (f + F // 2) % F, tokens],
-                    rhs=ident[:],
-                    is_transpose=True,
-                    start=False,
-                    stop=True,
-                )
-            nc.scalar.copy(out=summed[:, b, :], in_=bank[:])
-            if b % 2 == 1:
-                nc.sync.dma_start(out=outs[m][:, b - 1 : b + 1, t, :], in_=summed[:, b - 1 : b + 1, :])
 
-        def d_matmuls(t, half, i):
-            n = t * B + 2 * half + i
+        def d_matmuls(t, b):
+            n = t * B + b
             tokens = slice(n * P, (n + 1) * P)
             accs = []
             for m in range(2):
@@ -209,8 +220,8 @@ def tile_attention_pa_t_kernel(tc, x, cos, sin, Wq, Wk, out_0, out_1):
                 accs.append(project(x_codes[:, tokens], x_scales[:, tokens], w_codes[:, feats], w_scales[:, feats]))
             return accs
 
-        def d_products(t, half, i, accs):
-            straight = work.tile([P, 2, D], F32, tag="d_straight", bufs=4)
+        def d_products(t, b, accs):
+            straight = work.tile([P, 2, D], F32, tag="d_straight", bufs=5)
             crossed = work.tile([P, 2, D], F32, tag="d_crossed", bufs=3)
             by_half = "p (h j) -> p h j"
             for m, acc in enumerate(accs):
@@ -223,87 +234,93 @@ def tile_attention_pa_t_kernel(tc, x, cos, sin, Wq, Wk, out_0, out_1):
                 )
             nc.gpsimd.tensor_tensor(out=straight[:], in0=straight[:], in1=crossed[:], op=ADD)
             for m in range(2):
-                nc.sync.dma_start(out=outs[m][:, 2 * half + i, t, :], in_=straight[:, m, :])
+                nc.sync.dma_start(out=outs[m][:, b, t, :], in_=straight[:, m, :])
 
-        queues = {
-            "T": [(t, m) for t in T_POSITIONS for m in range(2)],
-            "D": [(t, half) for t in D_POSITIONS for half in range(2)],
+        units = {
+            "T": [(t, m, pair) for t in T_POSITIONS for m in range(2) for pair in range(2)],
+            "D": [(t, b) for t in D_POSITIONS for b in range(B)],
         }
         taken = {"T": 0, "D": 0}
         groups = []
         first_use = {}
-        for i, kind in enumerate(KINDS):
-            t, part = queues[kind][taken[kind]]
+        for kind in KINDS:
+            unit = units[kind][taken[kind]]
+            groups.append((kind, taken[kind], unit))
             taken[kind] += 1
-            first_use.setdefault(t, len(groups))
-            for half in range(2):
-                groups.append((kind, i, t, part, half))
+            first_use.setdefault(unit[0], len(groups) - 1)
 
-        prepare = []
+        prepare = [(0, "w", (0, 1)), (0, "w", (1, 0)), (0, "w", (1, 1))]
         for t in sorted(first_use, key=first_use.get):
             due = first_use[t] - 3
-            prepare += [(due, t, turn_x, (t, 0)), (due, t, turn_x, (t, 1))]
-            if t in T_POSITIONS:
-                prepare.append((due, t, turn_tables, (t,)))
-        left = {t: 3 if t in T_POSITIONS else 2 for t in first_use}
+            if t != T_POSITIONS[0]:
+                prepare += [(due, "x", (t, 0)), (due, "x", (t, 1))]
+                if t in T_POSITIONS:
+                    prepare.append((due, "table", (t,)))
         sums = []
         state = {"prepared": 0, "summed": 0}
         to_quantise = []
 
+        def prepare_piece(what, which, copy):
+            if what == "w":
+                turn_w(*which, copy)
+                to_quantise.append((quantise_w, which))
+            elif what == "table":
+                turn_tables(*which)
+            else:
+                t, half = which
+                if half == 0:
+                    negate_sin(t)
+                else:
+                    to_quantise.append((quantise_x, (t,)))
+                turn_x(t, half, copy)
+
+        def quantise_waiting():
+            for call, which in to_quantise:
+                call(*which)
+            to_quantise.clear()
+
         def next_prepare():
-            due, t, call, arguments = prepare[state["prepared"]]
+            due, what, which = prepare[state["prepared"]]
             state["prepared"] += 1
-            call(*arguments)
-            left[t] -= 1
-            if call == turn_x and arguments[1] == 1:
-                to_quantise.append(t)
-            if call == turn_x and arguments[1] == 0:
-                negate_sin(t)
+            prepare_piece(what, which, nc.scalar.copy)
 
         def next_sum():
-            call_arguments = sums[state["summed"]][1]
+            arguments = sums[state["summed"]][1]
             state["summed"] += 1
-            t_sums(*call_arguments)
+            t_sums(*arguments)
 
         def matmuls(g):
-            kind, i, t, part, half = groups[g]
-            return t_matmuls(t, part, half) if kind == "T" else d_matmuls(t, part, half)
+            kind, n, unit = groups[g]
+            return t_matmuls(*unit) if kind == "T" else d_matmuls(*unit)
 
-        prepare_w(0)
-        next_prepare()
-        next_prepare()
-        for t in to_quantise:
-            quantise_x(t)
-        to_quantise.clear()
-        next_prepare()
+        t = T_POSITIONS[0]
+        prepare_piece("w", (0, 0), nc.vector.tensor_copy)
+        prepare_piece("x", (t, 0), nc.scalar.copy)
+        quantise_waiting()
+        prepare_piece("x", (t, 1), nc.vector.tensor_copy)
+        quantise_waiting()
+        prepare_piece("table", (t,), nc.scalar.copy)
         accs = matmuls(0)
-        results = {}
-        for g, (kind, i, t, part, half) in enumerate(groups):
-            if g == 1:
-                prepare_w(1)
-            following = matmuls(g + 1) if g + 1 < len(groups) else []
+        next_prepare()
+        summed = None
+        for g, (kind, n, unit) in enumerate(groups):
             if kind == "T":
-                if half == 0:
-                    straight = work.tile([P, F, B * P], F32, tag="t_straight", bufs=3)
-                    crossed = work.tile([P, F, B * P], F32, tag="t_crossed", bufs=3)
-                    results[i] = (straight, crossed)
-                straight, crossed = results[i]
-                t_products(t, half, accs, straight, crossed, N_GPSIMD.get(i, 4))
-                if half == 1:
-                    summed = work.tile([P, B, D], F32, tag="t_summed", bufs=2)
-                    for b in range(B):
-                        sums.append((g + LAG, (t, part, b, straight, crossed, summed)))
+                t, m, pair = unit
+                straight, crossed = t_products(t, pair, accs, GPSIMD_BLOCKS[n % len(GPSIMD_BLOCKS)])
+                if pair == 0:
+                    summed = work.tile([P, B, 2, 2, P], F32, tag="t_summed", bufs=2)
+                for b in range(0, B, 2):
+                    sums.append((g + LAG, (t, m, pair, b, straight, crossed, summed)))
             else:
-                d_products(t, part, half, accs)
-            accs = following
-            for t in to_quantise:
-                quantise_x(t)
-            to_quantise.clear()
+                d_products(*unit, accs)
+            quantise_waiting()
+            if g + 1 < len(groups):
+                accs = matmuls(g + 1)
             count = 0
-            while state["prepared"] < len(prepare) and (count == 0 or prepare[state["prepared"]][0] <= g) and (prepare[state["prepared"]][0] <= g + 4):
+            while state["prepared"] < len(prepare) and count < CHUNKS[kind] and prepare[state["prepared"]][0] <= g + AHEAD * (count == 0):
                 next_prepare()
                 count += 1
-            while count < CHUNKS and state["summed"] < len(sums) and sums[state["summed"]][0] <= g:
+            while count < CHUNKS[kind] and state["summed"] < len(sums) and sums[state["summed"]][0] <= g:
                 next_sum()
                 count += 1
         while state["summed"] < len(sums):

@@ -17,11 +17,11 @@ HALF = D // 2
 T = S // P
 F = D // P
 
-KINDS = "TTTTDTDTDTTDTDTDTTDTDTDTTDTDTDTT"
+KINDS = "TTTT" + "DTDTDTT" * 4
 T_POSITIONS = (0, 2, 4, 6, 7)
 D_POSITIONS = (1, 3, 5)
 LAG = 3
-GPSIMD_BLOCKS = (2, 2, 2, 2, 1, 2, 1, 1, 2, 1, 1, 2, 1, 1, 2, 1, 1, 1, 0, 0)
+GPSIMD_BLOCKS = (2, 1, 1, 1, 1, 2, 1, 1, 1, 2, 1, 1, 1, 2, 1, 1, 1, 1, 0, 0)
 CHUNKS = {"T": 2, "D": 2}
 AHEAD = 4
 
@@ -37,6 +37,23 @@ def tile_attention_pa_t_kernel(tc, x, cos, sin, Wq, Wk, out_0, out_1):
         work = ctx.enter_context(tc.tile_pool(name="work", bufs=2))
         psum_acc = ctx.enter_context(tc.psum_pool(name="psum_acc", bufs=4))
         psum_tr = ctx.enter_context(tc.psum_pool(name="psum_tr", bufs=4))
+
+        units = {
+            "T": [(t, m, pair) for t in T_POSITIONS for m in range(2) for pair in range(2)],
+            "D": [(t, b) for t in D_POSITIONS for b in range(B)],
+        }
+        taken = {"T": 0, "D": 0}
+        groups = []
+        first_use = {}
+        for kind in KINDS:
+            unit = units[kind][taken[kind]]
+            groups.append((kind, taken[kind], unit))
+            taken[kind] += 1
+            first_use.setdefault(unit[0], len(groups) - 1)
+
+        by_use = sorted(first_use, key=first_use.get)
+        x_sets = [by_use[0:1], by_use[1:3], by_use[3:5], by_use[5:7], by_use[7:8]]
+        place = {t: i for i, t in enumerate(by_use)}
 
         x_view = x.rearrange("b (p t) d -> p b t d", t=T)
         cos_view = cos.rearrange("(p t) d -> p t d", t=T)
@@ -69,15 +86,14 @@ def tile_attention_pa_t_kernel(tc, x, cos, sin, Wq, Wk, out_0, out_1):
         load_x(0, 1)
         load_tables(0, 1)
         load_w(0, 1)
-        load_x(1, 2)
         load_w(1, 0)
         load_w(1, 1)
-        load_tables(1, 2)
-        load_x(2, 4)
-        load_tables(2, 4)
-        load_x(4, 6)
-        load_tables(4, 8)
-        load_x(6, 8)
+        load_x(1, 3)
+        load_tables(1, 3)
+        load_x(3, 5)
+        load_tables(3, 8)
+        load_x(5, 7)
+        load_x(7, 8)
 
         ident = keep.tile([P, P], F32)
         make_identity(nc, ident[:])
@@ -86,7 +102,7 @@ def tile_attention_pa_t_kernel(tc, x, cos, sin, Wq, Wk, out_0, out_1):
 
         def negate_sin(t):
             first = table_rows[t][1][:, 0:HALF]
-            nc.vector.tensor_scalar_mul(out=first, in0=first, scalar1=-1.0)
+            nc.scalar.mul(first, first, -1.0)
 
         def turn(rows_list, grouped, copy):
             bank = psum_tr.tile([P, 2, 2, P], F32, tag="tr")
@@ -123,14 +139,21 @@ def tile_attention_pa_t_kernel(tc, x, cos, sin, Wq, Wk, out_0, out_1):
         x_grouped = {}
 
         def turn_x(t, half, copy):
-            if half == 0:
-                x_grouped[t] = work.tile([P, B * P * 4], BF16, align_bytes=64, tag="x_grouped", bufs=3, name="x_grouped")
+            for members in x_sets:
+                if t == members[0] and half == 0:
+                    raw = work.tile([P, len(members) * B * P * 4], BF16, align_bytes=64, tag="x_grouped", bufs=2, name="x_grouped")
+                    for i, member in enumerate(members):
+                        x_grouped[member] = raw[:, i * B * P * 4 : (i + 1) * B * P * 4]
+                    x_grouped[members[0], "all"] = raw
             cols = slice(half * 2 * P * 4, (half + 1) * 2 * P * 4)
             turn([x_rows[t, 2 * half], x_rows[t, 2 * half + 1]], x_grouped[t][:, cols], copy)
 
-        def quantise_x(t):
-            cols = slice(t * B * P, (t + 1) * B * P)
-            nc.vector.quantize_mx(out=x_codes[:, cols].bitcast(FP8X4), scales=x_scales[:, cols], in_=x_grouped[t][:])
+        def quantise_x(members):
+            first = place[members[0]]
+            cols = slice(first * B * P, (first + len(members)) * B * P)
+            nc.vector.quantize_mx(
+                out=x_codes[:, cols].bitcast(FP8X4), scales=x_scales[:, cols], in_=x_grouped[members[0], "all"][:]
+            )
 
         tables = {}
 
@@ -159,7 +182,7 @@ def tile_attention_pa_t_kernel(tc, x, cos, sin, Wq, Wk, out_0, out_1):
 
         def t_matmuls(t, m, pair):
             accs = []
-            tokens = slice(t * B * P, (t + 1) * B * P)
+            tokens = slice(place[t] * B * P, (place[t] + 1) * B * P)
             for h in range(2):
                 block = m * D + (pair + 2 * h) * P
                 feats = slice(block, block + P)
@@ -212,7 +235,7 @@ def tile_attention_pa_t_kernel(tc, x, cos, sin, Wq, Wk, out_0, out_1):
                 )
 
         def d_matmuls(t, b):
-            n = t * B + b
+            n = place[t] * B + b
             tokens = slice(n * P, (n + 1) * P)
             accs = []
             for m in range(2):
@@ -236,26 +259,13 @@ def tile_attention_pa_t_kernel(tc, x, cos, sin, Wq, Wk, out_0, out_1):
             for m in range(2):
                 nc.sync.dma_start(out=outs[m][:, b, t, :], in_=straight[:, m, :])
 
-        units = {
-            "T": [(t, m, pair) for t in T_POSITIONS for m in range(2) for pair in range(2)],
-            "D": [(t, b) for t in D_POSITIONS for b in range(B)],
-        }
-        taken = {"T": 0, "D": 0}
-        groups = []
-        first_use = {}
-        for kind in KINDS:
-            unit = units[kind][taken[kind]]
-            groups.append((kind, taken[kind], unit))
-            taken[kind] += 1
-            first_use.setdefault(unit[0], len(groups) - 1)
-
         prepare = [(0, "w", (0, 1)), (0, "w", (1, 0)), (0, "w", (1, 1))]
-        for t in sorted(first_use, key=first_use.get):
-            due = first_use[t] - 3
-            if t != T_POSITIONS[0]:
-                prepare += [(due, "x", (t, 0)), (due, "x", (t, 1))]
+        for members in x_sets[1:]:
+            for t in members:
+                prepare += [(first_use[members[0]] - 3, "x", (t, half)) for half in range(2)]
+            for t in members:
                 if t in T_POSITIONS:
-                    prepare.append((due, "table", (t,)))
+                    prepare.append((first_use[t] - 2, "table", (t,)))
         sums = []
         state = {"prepared": 0, "summed": 0}
         to_quantise = []
@@ -271,7 +281,9 @@ def tile_attention_pa_t_kernel(tc, x, cos, sin, Wq, Wk, out_0, out_1):
                 if half == 0:
                     negate_sin(t)
                 else:
-                    to_quantise.append((quantise_x, (t,)))
+                    for members in x_sets:
+                        if t == members[-1]:
+                            to_quantise.append((quantise_x, (members,)))
                 turn_x(t, half, copy)
 
         def quantise_waiting():
@@ -313,7 +325,8 @@ def tile_attention_pa_t_kernel(tc, x, cos, sin, Wq, Wk, out_0, out_1):
                     sums.append((g + LAG, (t, m, pair, b, straight, crossed, summed)))
             else:
                 d_products(*unit, accs)
-            quantise_waiting()
+            if g < 4 or (g - 4) % 7 == 6:
+                quantise_waiting()
             if g + 1 < len(groups):
                 accs = matmuls(g + 1)
             count = 0

@@ -21,7 +21,7 @@ KINDS = "TTTT" + "DTDTDTT" * 4
 T_POSITIONS = (0, 2, 4, 6, 7)
 D_POSITIONS = (1, 3, 5)
 LAG = 3
-GPSIMD_BLOCKS = (2, 1, 1, 1, 1, 2, 1, 1, 1, 2, 1, 1, 1, 2, 1, 1, 1, 1, 0, 0)
+GPSIMD_BLOCKS = (1, 1, 1, 1, 1, 2, 1, 1, 1, 2, 1, 1, 1, 2, 1, 1, 1, 1, 0, 0)
 CHUNKS = {"T": 2, "D": 2}
 AHEAD = 4
 
@@ -52,7 +52,7 @@ def tile_attention_pa_t_kernel(tc, x, cos, sin, Wq, Wk, out_0, out_1):
             first_use.setdefault(unit[0], len(groups) - 1)
 
         by_use = sorted(first_use, key=first_use.get)
-        x_sets = [by_use[0:1], by_use[1:3], by_use[3:5], by_use[5:7], by_use[7:8]]
+        x_sets = [by_use[0:1], by_use[1:2], by_use[2:3], by_use[3:5], by_use[5:7], by_use[7:8]]
         place = {t: i for i, t in enumerate(by_use)}
 
         x_view = x.rearrange("b (p t) d -> p b t d", t=T)
@@ -75,12 +75,15 @@ def tile_attention_pa_t_kernel(tc, x, cos, sin, Wq, Wk, out_0, out_1):
                         x_rows[t, b + i] = x_sb[:, i, t - t0, :]
 
         def load_tables(t0, t1):
-            cos_sb = keep.tile([P, t1 - t0, D], BF16, name="cos_sb%d" % t0)
-            sin_sb = keep.tile([P, t1 - t0, D], BF16, name="sin_sb%d" % t0)
-            nc.sync.dma_start(out=cos_sb[:], in_=cos_view[:, t0:t1, :])
-            nc.sync.dma_start(out=sin_sb[:], in_=sin_view[:, t0:t1, :])
+            table_sb = keep.tile([P, t1 - t0, 2, D], BF16, name="table_sb%d" % t0)
+            nc.sync.dma_start(out=table_sb[:, :, 0, :], in_=cos_view[:, t0:t1, :])
+            for h in range(2):
+                nc.sync.dma_start(
+                    out=table_sb[:, :, 1, (1 - h) * HALF : (2 - h) * HALF],
+                    in_=sin_view[:, t0:t1, h * HALF : (h + 1) * HALF],
+                )
             for t in range(t0, t1):
-                table_rows[t] = (cos_sb[:, t - t0, :], sin_sb[:, t - t0, :])
+                table_rows[t] = table_sb[:, t - t0]
 
         load_w(0, 0)
         load_x(0, 1)
@@ -101,7 +104,7 @@ def tile_attention_pa_t_kernel(tc, x, cos, sin, Wq, Wk, out_0, out_1):
         make_identity(nc, ident_b[:])
 
         def negate_sin(t):
-            first = table_rows[t][1][:, 0:HALF]
+            first = table_rows[t][:, 1, HALF:D]
             nc.scalar.mul(first, first, -1.0)
 
         def turn(rows_list, grouped, copy):
@@ -141,7 +144,7 @@ def tile_attention_pa_t_kernel(tc, x, cos, sin, Wq, Wk, out_0, out_1):
         def turn_x(t, half, copy):
             for members in x_sets:
                 if t == members[0] and half == 0:
-                    raw = work.tile([P, len(members) * B * P * 4], BF16, align_bytes=64, tag="x_grouped", bufs=2, name="x_grouped")
+                    raw = work.tile([P, len(members) * B * P * 4], BF16, align_bytes=64, tag="x_grouped", bufs=3, name="x_grouped")
                     for i, member in enumerate(members):
                         x_grouped[member] = raw[:, i * B * P * 4 : (i + 1) * B * P * 4]
                     x_grouped[members[0], "all"] = raw
@@ -159,10 +162,9 @@ def tile_attention_pa_t_kernel(tc, x, cos, sin, Wq, Wk, out_0, out_1):
 
         def turn_tables(t):
             bank = psum_tr.tile([P, 2, F, P], BF16, tag="tr")
-            for k, table in enumerate(table_rows[t]):
+            for k in range(2):
                 for f in range(F):
-                    source = f if k == 0 else (f + F // 2) % F
-                    nc.tensor.transpose(bank[:, k, f, :], table[:, source * P : (source + 1) * P], ident_b[:])
+                    nc.tensor.transpose(bank[:, k, f, :], table_rows[t][:, k, f * P : (f + 1) * P], ident_b[:])
             turned = keep.tile([P, 2, F, P], BF16, name="turned%d" % t)
             nc.scalar.copy(out=turned[:], in_=bank[:])
             tables[t] = turned[:].rearrange("p k (h c) s -> p k h c s", h=2)
@@ -190,43 +192,40 @@ def tile_attention_pa_t_kernel(tc, x, cos, sin, Wq, Wk, out_0, out_1):
             return accs
 
         def t_products(t, pair, accs, n_gpsimd):
-            straight = work.tile([P, 2, B * P], F32, tag="t_straight", bufs=5)
-            crossed = work.tile([P, 2, B * P], F32, tag="t_crossed", bufs=5)
+            products = work.tile([P, 2, 2, B * P], F32, tag="t_products", bufs=5)
             by_batch = "p (b s) -> p b s"
             if n_gpsimd:
                 copied = work.tile([P, 2, B * P], F32, tag="t_copied", bufs=4)
             for h, acc in enumerate(accs):
-                mine = h < n_gpsimd
-                for k, dest in enumerate((straight, crossed)):
-                    if k == 0 or not mine:
-                        nc.vector.tensor_tensor(
-                            out=dest[:, h, :].rearrange(by_batch, b=B),
-                            in0=acc[:].rearrange(by_batch, b=B),
-                            in1=tables[t][:, k, h, pair, :].unsqueeze(1).to_broadcast([P, B, P]),
-                            op=MULT,
-                        )
-                if mine:
+                n_here = 1 if h < n_gpsimd else 2
+                nc.vector.tensor_tensor(
+                    out=products[:, h, 0:n_here, :].rearrange("p k (b s) -> p k b s", b=B),
+                    in0=acc[:].rearrange(by_batch, b=B).unsqueeze(1).to_broadcast([P, n_here, B, P]),
+                    in1=tables[t][:, 0:n_here, h, pair, :].unsqueeze(2).to_broadcast([P, n_here, B, P]),
+                    op=MULT,
+                )
+                if n_here == 1:
                     nc.scalar.copy(out=copied[:, h, :], in_=acc[:])
             if n_gpsimd:
                 by_batch = "p h (b s) -> p h b s"
                 nc.gpsimd.tensor_tensor(
-                    out=crossed[:, 0:n_gpsimd, :].rearrange(by_batch, b=B),
+                    out=products[:, 0:n_gpsimd, 1, :].rearrange(by_batch, b=B),
                     in0=copied[:, 0:n_gpsimd, :].rearrange(by_batch, b=B),
                     in1=tables[t][:, 1, 0:n_gpsimd, pair, :].unsqueeze(2).to_broadcast([P, n_gpsimd, B, P]),
                     op=MULT,
                 )
-            return straight, crossed
+            return products
 
-        def t_sums(t, m, pair, b, straight, crossed, summed):
+        def t_sums(t, m, pair, b, products, summed):
             bank = psum_tr.tile([P, 2, 2, P], F32, tag="tr")
             for i in range(2):
                 tokens = slice((b + i) * P, (b + i + 1) * P)
                 for h in range(2):
                     nc.tensor.matmul(
-                        bank[:, i, h, :], lhsT=straight[:, h, tokens], rhs=ident[:], is_transpose=True, start=True, stop=False
+                        bank[:, i, h, :], lhsT=products[:, h, 0, tokens], rhs=ident[:], is_transpose=True, start=True, stop=False
                     )
                     nc.tensor.matmul(
-                        bank[:, i, h, :], lhsT=crossed[:, 1 - h, tokens], rhs=ident[:], is_transpose=True, start=False, stop=True
+                        bank[:, i, h, :], lhsT=products[:, 1 - h, 1, tokens], rhs=ident[:], is_transpose=True, start=False, stop=True
                     )
             nc.scalar.copy(out=summed[:, b : b + 2, :, pair, :], in_=bank[:])
             if pair == 1:
@@ -244,20 +243,17 @@ def tile_attention_pa_t_kernel(tc, x, cos, sin, Wq, Wk, out_0, out_1):
             return accs
 
         def d_products(t, b, accs):
-            straight = work.tile([P, 2, D], F32, tag="d_straight", bufs=5)
-            crossed = work.tile([P, 2, D], F32, tag="d_crossed", bufs=3)
-            by_half = "p (h j) -> p h j"
+            products = work.tile([P, 2, 2, D], F32, tag="d_products", bufs=4)
             for m, acc in enumerate(accs):
-                nc.vector.tensor_tensor(out=straight[:, m, :], in0=acc[:], in1=table_rows[t][0], op=MULT)
                 nc.vector.tensor_tensor(
-                    out=crossed[:, m, :].rearrange(by_half, h=2),
-                    in0=acc[:].rearrange(by_half, h=2)[:, ::-1, :],
-                    in1=table_rows[t][1].rearrange(by_half, h=2),
-                    op=MULT,
+                    out=products[:, m], in0=acc[:].unsqueeze(1).to_broadcast([P, 2, D]), in1=table_rows[t], op=MULT
                 )
-            nc.gpsimd.tensor_tensor(out=straight[:], in0=straight[:], in1=crossed[:], op=ADD)
+            by_half = "p m (h j) -> p m h j"
+            straight = products[:, :, 0, :].rearrange(by_half, h=2)
+            crossed = products[:, :, 1, :].rearrange(by_half, h=2)
+            nc.gpsimd.tensor_tensor(out=straight, in0=straight, in1=crossed[:, :, ::-1, :], op=ADD)
             for m in range(2):
-                nc.sync.dma_start(out=outs[m][:, b, t, :], in_=straight[:, m, :])
+                nc.sync.dma_start(out=outs[m][:, b, t, :], in_=products[:, m, 0, :])
 
         prepare = [(0, "w", (0, 1)), (0, "w", (1, 0)), (0, "w", (1, 1))]
         for members in x_sets[1:]:
@@ -312,20 +308,21 @@ def tile_attention_pa_t_kernel(tc, x, cos, sin, Wq, Wk, out_0, out_1):
         prepare_piece("x", (t, 1), nc.vector.tensor_copy)
         quantise_waiting()
         prepare_piece("table", (t,), nc.scalar.copy)
-        accs = matmuls(0)
         next_prepare()
+        quantise_waiting()
+        accs = matmuls(0)
         summed = None
         for g, (kind, n, unit) in enumerate(groups):
             if kind == "T":
                 t, m, pair = unit
-                straight, crossed = t_products(t, pair, accs, GPSIMD_BLOCKS[n % len(GPSIMD_BLOCKS)])
+                products = t_products(t, pair, accs, GPSIMD_BLOCKS[n % len(GPSIMD_BLOCKS)])
                 if pair == 0:
                     summed = work.tile([P, B, 2, 2, P], F32, tag="t_summed", bufs=2)
                 for b in range(0, B, 2):
-                    sums.append((g + LAG, (t, m, pair, b, straight, crossed, summed)))
+                    sums.append((g + LAG, (t, m, pair, b, products, summed)))
             else:
                 d_products(*unit, accs)
-            if g < 4 or (g - 4) % 7 == 6:
+            if g < 6 or (g - 4) % 7 == 6:
                 quantise_waiting()
             if g + 1 < len(groups):
                 accs = matmuls(g + 1)

@@ -17,11 +17,11 @@ HALF = D // 2
 T = S // P
 F = D // P
 
-KINDS = "TTTT" + "DTDTDTT" * 4
+KINDS = "TTTT" + "DTDTDTT" * 3 + "DTTDTTD"
 T_POSITIONS = (0, 2, 4, 6, 7)
 D_POSITIONS = (1, 3, 5)
-LAG = 3
-GPSIMD_BLOCKS = (1, 1, 1, 1, 1, 2, 1, 1, 1, 2, 1, 1, 1, 2, 1, 1, 1, 1, 0, 0)
+LAG = 2
+GPSIMD_BLOCKS = (1, 1, 1, 1, 1, 2, 1, 1, 1, 2, 1, 1, 1, 2, 1, 1, 1, 1, 1, 0)
 CHUNKS = {"T": 2, "D": 2}
 AHEAD = 4
 
@@ -60,52 +60,59 @@ def tile_attention_pa_t_kernel(tc, x, cos, sin, Wq, Wk, out_0, out_1):
         sin_view = sin.rearrange("(p t) d -> p t d", t=T)
         w_rows, x_rows, table_rows = {}, {}, {}
 
-        def load_w(m, pair):
-            w_sb = keep.tile([P, 2, D], BF16, name="w_sb%d%d" % (m, pair))
-            nc.sync.dma_start(out=w_sb[:], in_=(Wq, Wk)[m].rearrange("(h c p) k -> p h c k", h=2, p=P)[:, :, pair, :])
+        def load_w(m, pairs):
+            w_sb = keep.tile([P, 2, len(pairs), D], BF16, name="w_sb%d%d" % (m, pairs[0]))
+            w_view = (Wq, Wk)[m].rearrange("(h c p) k -> p h c k", h=2, p=P)
             for h in range(2):
-                w_rows[m, pair + 2 * h] = w_sb[:, h, :]
+                w_rows_h = w_view[:, h, pairs[0] : pairs[-1] + 1, :]
+                nc.sync.dma_start(out=w_sb[:, h], in_=w_rows_h)
+                for i, pair in enumerate(pairs):
+                    w_rows[m, pair + 2 * h] = w_sb[:, h, i, :]
 
-        def load_x(t0, t1):
-            for b in range(0, B, 2):
-                x_sb = keep.tile([P, 2, t1 - t0, D], BF16, name="x_sb%d%d" % (t0, b))
-                nc.sync.dma_start(out=x_sb[:], in_=x_view[:, b : b + 2, t0:t1, :])
-                for t in range(t0, t1):
-                    for i in range(2):
-                        x_rows[t, b + i] = x_sb[:, i, t - t0, :]
+        def load_x(t0, t1, b0, b1):
+            x_sb = keep.tile([P, b1 - b0, t1 - t0, D], BF16, name="x_sb%d%d" % (t0, b0))
+            nc.sync.dma_start(out=x_sb[:], in_=x_view[:, b0:b1, t0:t1, :])
+            for t in range(t0, t1):
+                for b in range(b0, b1):
+                    x_rows[t, b] = x_sb[:, b - b0, t - t0, :]
 
         def load_tables(t0, t1):
-            table_sb = keep.tile([P, t1 - t0, 2, D], BF16, name="table_sb%d" % t0)
-            nc.sync.dma_start(out=table_sb[:, :, 0, :], in_=cos_view[:, t0:t1, :])
-            for h in range(2):
-                nc.sync.dma_start(
-                    out=table_sb[:, :, 1, (1 - h) * HALF : (2 - h) * HALF],
-                    in_=sin_view[:, t0:t1, h * HALF : (h + 1) * HALF],
-                )
+            cos_sb = keep.tile([P, t1 - t0, D], BF16, name="cos_sb%d" % t0)
+            sin_sb = keep.tile([P, t1 - t0, D], BF16, name="sin_sb%d" % t0)
+            nc.sync.dma_start(out=cos_sb[:], in_=cos_view[:, t0:t1, :])
+            nc.sync.dma_start(out=sin_sb[:], in_=sin_view[:, t0:t1, :])
             for t in range(t0, t1):
-                table_rows[t] = table_sb[:, t - t0]
+                table_rows[t] = (cos_sb[:, t - t0, :], sin_sb[:, t - t0, :])
 
-        load_w(0, 0)
-        load_x(0, 1)
+        load_w(0, [0])
+        load_x(0, 1, 0, 2)
+        load_x(0, 1, 2, 4)
         load_tables(0, 1)
-        load_w(0, 1)
-        load_w(1, 0)
-        load_w(1, 1)
-        load_x(1, 3)
-        load_tables(1, 3)
-        load_x(3, 5)
-        load_tables(3, 8)
-        load_x(5, 7)
-        load_x(7, 8)
+        load_w(0, [1])
+        load_w(1, [0, 1])
+        load_x(1, 3, 0, 4)
+        load_tables(1, 8)
+        load_x(3, 5, 0, 4)
+        load_x(5, 7, 0, 4)
+        load_x(7, 8, 0, 4)
 
         ident = keep.tile([P, P], F32)
         make_identity(nc, ident[:])
         ident_b = keep.tile([P, P], BF16)
         make_identity(nc, ident_b[:])
 
-        def negate_sin(t):
-            first = table_rows[t][:, 1, HALF:D]
-            nc.scalar.mul(first, first, -1.0)
+        def sort_tables(t):
+            cos_row, sin_row = table_rows[t]
+            if t in T_POSITIONS:
+                nc.scalar.mul(sin_row[:, 0:HALF], sin_row[:, 0:HALF], -1.0)
+            else:
+                d_table = keep.tile([P, 2, D], BF16, name="d_table%d" % t)
+                nc.scalar.copy(out=d_table[:, 0, :], in_=cos_row)
+                nc.scalar.copy(out=d_table[:, 1, 0:HALF], in_=sin_row[:, HALF:D])
+                nc.scalar.mul(d_table[:, 1, HALF:D], sin_row[:, 0:HALF], -1.0)
+                d_tables[t] = d_table
+
+        d_tables = {}
 
         def turn(rows_list, grouped, copy):
             bank = psum_tr.tile([P, 2, 2, P], F32, tag="tr")
@@ -162,9 +169,10 @@ def tile_attention_pa_t_kernel(tc, x, cos, sin, Wq, Wk, out_0, out_1):
 
         def turn_tables(t):
             bank = psum_tr.tile([P, 2, F, P], BF16, tag="tr")
-            for k in range(2):
+            for k, row in enumerate(table_rows[t]):
                 for f in range(F):
-                    nc.tensor.transpose(bank[:, k, f, :], table_rows[t][:, k, f * P : (f + 1) * P], ident_b[:])
+                    source = (f + k * F // 2) % F
+                    nc.tensor.transpose(bank[:, k, f, :], row[:, source * P : (source + 1) * P], ident_b[:])
             turned = keep.tile([P, 2, F, P], BF16, name="turned%d" % t)
             nc.scalar.copy(out=turned[:], in_=bank[:])
             tables[t] = turned[:].rearrange("p k (h c) s -> p k h c s", h=2)
@@ -242,18 +250,23 @@ def tile_attention_pa_t_kernel(tc, x, cos, sin, Wq, Wk, out_0, out_1):
                 accs.append(project(x_codes[:, tokens], x_scales[:, tokens], w_codes[:, feats], w_scales[:, feats]))
             return accs
 
-        def d_products(t, b, accs):
-            products = work.tile([P, 2, 2, D], F32, tag="d_products", bufs=4)
-            for m, acc in enumerate(accs):
-                nc.vector.tensor_tensor(
-                    out=products[:, m], in0=acc[:].unsqueeze(1).to_broadcast([P, 2, D]), in1=table_rows[t], op=MULT
-                )
+        def d_products(t, b, accs, last):
+            products = work.tile([P, 2, 2, D], F32, tag="d_products", bufs=3)
             by_half = "p m (h j) -> p m h j"
             straight = products[:, :, 0, :].rearrange(by_half, h=2)
-            crossed = products[:, :, 1, :].rearrange(by_half, h=2)
-            nc.gpsimd.tensor_tensor(out=straight, in0=straight, in1=crossed[:, :, ::-1, :], op=ADD)
+            crossed = products[:, :, 1, :].rearrange(by_half, h=2)[:, :, ::-1, :]
+            for m, acc in enumerate(accs):
+                nc.vector.tensor_tensor(
+                    out=products[:, m], in0=acc[:].unsqueeze(1).to_broadcast([P, 2, D]), in1=d_tables[t][:], op=MULT
+                )
+                if last and m == 0:
+                    nc.gpsimd.tensor_tensor(out=straight[:, 0], in0=straight[:, 0], in1=crossed[:, 0], op=ADD)
+            if last:
+                nc.vector.tensor_tensor(out=straight[:, 1], in0=straight[:, 1], in1=crossed[:, 1], op=ADD)
+            else:
+                nc.gpsimd.tensor_tensor(out=straight, in0=straight, in1=crossed, op=ADD)
             for m in range(2):
-                nc.sync.dma_start(out=outs[m][:, b, t, :], in_=products[:, m, 0, :])
+                stores.append((m, b, t, products))
 
         prepare = [(0, "w", (0, 1)), (0, "w", (1, 0)), (0, "w", (1, 1))]
         for members in x_sets[1:]:
@@ -263,6 +276,14 @@ def tile_attention_pa_t_kernel(tc, x, cos, sin, Wq, Wk, out_0, out_1):
                 if t in T_POSITIONS:
                     prepare.append((first_use[t] - 2, "table", (t,)))
         sums = []
+        stores = []
+
+        def store_waiting(n):
+            while len(stores) > n:
+                m, b, t, products = stores[0]
+                stores.remove(stores[0])
+                nc.sync.dma_start(out=outs[m][:, b, t, :], in_=products[:, m, 0, :])
+
         state = {"prepared": 0, "summed": 0}
         to_quantise = []
 
@@ -275,7 +296,7 @@ def tile_attention_pa_t_kernel(tc, x, cos, sin, Wq, Wk, out_0, out_1):
             else:
                 t, half = which
                 if half == 0:
-                    negate_sin(t)
+                    sort_tables(t)
                 else:
                     for members in x_sets:
                         if t == members[-1]:
@@ -321,7 +342,7 @@ def tile_attention_pa_t_kernel(tc, x, cos, sin, Wq, Wk, out_0, out_1):
                 for b in range(0, B, 2):
                     sums.append((g + LAG, (t, m, pair, b, products, summed)))
             else:
-                d_products(*unit, accs)
+                d_products(*unit, accs, g + 1 == len(groups))
             if g < 6 or (g - 4) % 7 == 6:
                 quantise_waiting()
             if g + 1 < len(groups):
@@ -333,5 +354,6 @@ def tile_attention_pa_t_kernel(tc, x, cos, sin, Wq, Wk, out_0, out_1):
             while count < CHUNKS[kind] and state["summed"] < len(sums) and sums[state["summed"]][0] <= g:
                 next_sum()
                 count += 1
+            store_waiting(2 * 0 if g + 1 < len(groups) else 0)
         while state["summed"] < len(sums):
             next_sum()

from contextlib import ExitStack

import concourse.mybir as mybir
from concourse.masks import make_identity

F32 = mybir.dt.float32
BF16 = mybir.dt.bfloat16
U32 = mybir.dt.uint32
U8 = mybir.dt.uint8
FP8X4 = mybir.dt.float8_e4m3fn_x4
MULT = mybir.AluOpType.mult
ADD = mybir.AluOpType.add

P = 128
B, S, D = 4, 1024, 512
HALF = D // 2
T = S // P
F = D // P

KINDS = "TTTT" + "DTDTDTT" * 3 + "DTTDTTD"
T_POSITIONS = (0, 2, 4, 6, 7)
D_POSITIONS = (1, 3, 5)
LAG = 2
GPSIMD_BLOCKS = (1, 1, 1, 1, 1, 2, 1, 1, 1, 2, 1, 1, 1, 2, 1, 1, 1, 1, 1, 0)
CHUNKS = {"T": 2, "D": 2}
AHEAD = 4

FLOPS = 2 * B * S * D * (2 * D)


def tile_attention_pa_t_kernel(tc, x, cos, sin, Wq, Wk, out_0, out_1):
    nc = tc.nc
    outs = [o.rearrange("b (p t) d -> p b t d", t=T) for o in (out_0, out_1)]
    with ExitStack() as ctx:
        ctx.enter_context(tc.manual_schedule())
        keep = ctx.enter_context(tc.tile_pool(name="keep", bufs=1))
        work = ctx.enter_context(tc.tile_pool(name="work", bufs=2))
        psum_acc = ctx.enter_context(tc.psum_pool(name="psum_acc", bufs=4))
        psum_tr = ctx.enter_context(tc.psum_pool(name="psum_tr", bufs=4))

        units = {
            "T": [(t, m, pair) for t in T_POSITIONS for m in range(2) for pair in range(2)],
            "D": [(t, b) for t in D_POSITIONS for b in range(B)],
        }
        taken = {"T": 0, "D": 0}
        groups = []
        first_use = {}
        for kind in KINDS:
            unit = units[kind][taken[kind]]
            groups.append((kind, taken[kind], unit))
            taken[kind] += 1
            first_use.setdefault(unit[0], len(groups) - 1)

        by_use = sorted(first_use, key=first_use.get)
        x_sets = [by_use[0:1], by_use[1:2], by_use[2:3], by_use[3:5], by_use[5:7], by_use[7:8]]
        place = {t: i for i, t in enumerate(by_use)}

        x_view = x.rearrange("b (p t) d -> p b t d", t=T)
        cos_view = cos.rearrange("(p t) d -> p t d", t=T)
        sin_view = sin.rearrange("(p t) d -> p t d", t=T)
        w_rows, x_rows, table_rows = {}, {}, {}

        def load_w(m, pairs):
            w_sb = keep.tile([P, 2, len(pairs), D], BF16, name="w_sb%d%d" % (m, pairs[0]))
            w_view = (Wq, Wk)[m].rearrange("(h c p) k -> p h c k", h=2, p=P)
            for h in range(2):
                w_rows_h = w_view[:, h, pairs[0] : pairs[-1] + 1, :]
                nc.sync.dma_start(out=w_sb[:, h], in_=w_rows_h)
                for i, pair in enumerate(pairs):
                    w_rows[m, pair + 2 * h] = w_sb[:, h, i, :]

        def load_x(t0, t1, b0, b1):
            x_sb = keep.tile([P, b1 - b0, t1 - t0, D], BF16, name="x_sb%d%d" % (t0, b0))
            nc.sync.dma_start(out=x_sb[:], in_=x_view[:, b0:b1, t0:t1, :])
            for t in range(t0, t1):
                for b in range(b0, b1):
                    x_rows[t, b] = x_sb[:, b - b0, t - t0, :]

        def load_tables(t0, t1):
            cos_sb = keep.tile([P, t1 - t0, D], BF16, name="cos_sb%d" % t0)
            sin_sb = keep.tile([P, t1 - t0, D], BF16, name="sin_sb%d" % t0)
            nc.sync.dma_start(out=cos_sb[:], in_=cos_view[:, t0:t1, :])
            nc.sync.dma_start(out=sin_sb[:], in_=sin_view[:, t0:t1, :])
            for t in range(t0, t1):
                table_rows[t] = (cos_sb[:, t - t0, :], sin_sb[:, t - t0, :])

        load_w(0, [0])
        load_x(0, 1, 0, 2)
        load_x(0, 1, 2, 4)
        load_tables(0, 1)
        load_w(0, [1])
        load_w(1, [0, 1])
        load_x(1, 3, 0, 4)
        load_tables(1, 8)
        load_x(3, 5, 0, 4)
        load_x(5, 7, 0, 4)
        load_x(7, 8, 0, 4)

        ident = keep.tile([P, P], F32)
        make_identity(nc, ident[:])
        ident_b = keep.tile([P, P], BF16)
        make_identity(nc, ident_b[:])

        def sort_tables(t):
            cos_row, sin_row = table_rows[t]
            if t in T_POSITIONS:
                nc.scalar.mul(sin_row[:, 0:HALF], sin_row[:, 0:HALF], -1.0)
            else:
                d_table = keep.tile([P, 2, D], BF16, name="d_table%d" % t)
                nc.scalar.copy(out=d_table[:, 0, :], in_=cos_row)
                nc.scalar.copy(out=d_table[:, 1, 0:HALF], in_=sin_row[:, HALF:D])
                nc.scalar.mul(d_table[:, 1, HALF:D], sin_row[:, 0:HALF], -1.0)
                d_tables[t] = d_table

        d_tables = {}

        def turn(rows_list, grouped, copy):
            bank = psum_tr.tile([P, 2, 2, P], F32, tag="tr")
            for j, rows in enumerate(rows_list):
                words = rows.bitcast(F32)
                for u in range(2):
                    nc.tensor.transpose(bank[:, j, u, :], words[:, u : 2 * P : 2], ident[:])
            copy(
                out=grouped.bitcast(F32).rearrange("p (i r u) -> p i r u", i=2, u=2),
                in_=bank[:].rearrange("p i u r -> p i r u"),
            )

        w_codes = keep.tile([P, 2 * D], U32, align_bytes=64)
        w_scales = keep.tile([P, 2 * D], U8, align_bytes=64)
        x_codes = keep.tile([P, T * B * P], U32, align_bytes=64)
        x_scales = keep.tile([P, T * B * P], U8, align_bytes=64)

        w_grouped = {}

        def turn_w(m, pair, copy):
            w_grouped[m, pair] = work.tile([P, 2 * P * 4], BF16, align_bytes=64, tag="w_grouped", bufs=3, name="w_grouped")
            turn([w_rows[m, pair], w_rows[m, pair + 2]], w_grouped[m, pair][:], copy)

        def quantise_w(m, pair):
            for h in range(2):
                block = m * D + (pair + 2 * h) * P
                cols = slice(block, block + P)
                nc.vector.quantize_mx(
                    out=w_codes[:, cols].bitcast(FP8X4),
                    scales=w_scales[:, cols],
                    in_=w_grouped[m, pair][:, h * P * 4 : (h + 1) * P * 4],
                )

        x_grouped = {}

        def turn_x(t, half, copy):
            for members in x_sets:
                if t == members[0] and half == 0:
                    raw = work.tile([P, len(members) * B * P * 4], BF16, align_bytes=64, tag="x_grouped", bufs=3, name="x_grouped")
                    for i, member in enumerate(members):
                        x_grouped[member] = raw[:, i * B * P * 4 : (i + 1) * B * P * 4]
                    x_grouped[members[0], "all"] = raw
            cols = slice(half * 2 * P * 4, (half + 1) * 2 * P * 4)
            turn([x_rows[t, 2 * half], x_rows[t, 2 * half + 1]], x_grouped[t][:, cols], copy)

        def quantise_x(members):
            first = place[members[0]]
            cols = slice(first * B * P, (first + len(members)) * B * P)
            nc.vector.quantize_mx(
                out=x_codes[:, cols].bitcast(FP8X4), scales=x_scales[:, cols], in_=x_grouped[members[0], "all"][:]
            )

        tables = {}

        def turn_tables(t):
            bank = psum_tr.tile([P, 2, F, P], BF16, tag="tr")
            for k, row in enumerate(table_rows[t]):
                for f in range(F):
                    source = (f + k * F // 2) % F
                    nc.tensor.transpose(bank[:, k, f, :], row[:, source * P : (source + 1) * P], ident_b[:])
            turned = keep.tile([P, 2, F, P], BF16, name="turned%d" % t)
            nc.scalar.copy(out=turned[:], in_=bank[:])
            tables[t] = turned[:].rearrange("p k (h c) s -> p k h c s", h=2)

        def project(lhs, lhs_scale, rhs, rhs_scale):
            acc = psum_acc.tile([P, D], F32, tag="acc")
            nc.tensor.matmul_mx(
                out=acc[:],
                lhsT=lhs.bitcast(FP8X4),
                lhsT_scale=lhs_scale,
                rhs=rhs.bitcast(FP8X4),
                rhs_scale=rhs_scale,
                start=True,
                stop=True,
            )
            return acc

        def t_matmuls(t, m, pair):
            accs = []
            tokens = slice(place[t] * B * P, (place[t] + 1) * B * P)
            for h in range(2):
                block = m * D + (pair + 2 * h) * P
                feats = slice(block, block + P)
                accs.append(project(w_codes[:, feats], w_scales[:, feats], x_codes[:, tokens], x_scales[:, tokens]))
            return accs

        def t_products(t, pair, accs, n_gpsimd):
            products = work.tile([P, 2, 2, B * P], F32, tag="t_products", bufs=5)
            by_batch = "p (b s) -> p b s"
            if n_gpsimd:
                copied = work.tile([P, 2, B * P], F32, tag="t_copied", bufs=4)
            for h, acc in enumerate(accs):
                n_here = 1 if h < n_gpsimd else 2
                nc.vector.tensor_tensor(
                    out=products[:, h, 0:n_here, :].rearrange("p k (b s) -> p k b s", b=B),
                    in0=acc[:].rearrange(by_batch, b=B).unsqueeze(1).to_broadcast([P, n_here, B, P]),
                    in1=tables[t][:, 0:n_here, h, pair, :].unsqueeze(2).to_broadcast([P, n_here, B, P]),
                    op=MULT,
                )
                if n_here == 1:
                    nc.scalar.copy(out=copied[:, h, :], in_=acc[:])
            if n_gpsimd:
                by_batch = "p h (b s) -> p h b s"
                nc.gpsimd.tensor_tensor(
                    out=products[:, 0:n_gpsimd, 1, :].rearrange(by_batch, b=B),
                    in0=copied[:, 0:n_gpsimd, :].rearrange(by_batch, b=B),
                    in1=tables[t][:, 1, 0:n_gpsimd, pair, :].unsqueeze(2).to_broadcast([P, n_gpsimd, B, P]),
                    op=MULT,
                )
            return products

        def t_sums(t, m, pair, b, products, summed):
            bank = psum_tr.tile([P, 2, 2, P], F32, tag="tr")
            for i in range(2):
                tokens = slice((b + i) * P, (b + i + 1) * P)
                for h in range(2):
                    nc.tensor.matmul(
                        bank[:, i, h, :], lhsT=products[:, h, 0, tokens], rhs=ident[:], is_transpose=True, start=True, stop=False
                    )
                    nc.tensor.matmul(
                        bank[:, i, h, :], lhsT=products[:, 1 - h, 1, tokens], rhs=ident[:], is_transpose=True, start=False, stop=True
                    )
            nc.scalar.copy(out=summed[:, b : b + 2, :, pair, :], in_=bank[:])
            if pair == 1:
                nc.sync.dma_start(
                    out=outs[m][:, b : b + 2, t, :], in_=summed[:, b : b + 2].rearrange("p b h c j -> p b (h c j)")
                )

        def d_matmuls(t, b):
            n = place[t] * B + b
            tokens = slice(n * P, (n + 1) * P)
            accs = []
            for m in range(2):
                feats = slice(m * D, (m + 1) * D)
                accs.append(project(x_codes[:, tokens], x_scales[:, tokens], w_codes[:, feats], w_scales[:, feats]))
            return accs

        def d_products(t, b, accs, last):
            products = work.tile([P, 2, 2, D], F32, tag="d_products", bufs=3)
            by_half = "p m (h j) -> p m h j"
            straight = products[:, :, 0, :].rearrange(by_half, h=2)
            crossed = products[:, :, 1, :].rearrange(by_half, h=2)[:, :, ::-1, :]
            for m, acc in enumerate(accs):
                nc.vector.tensor_tensor(
                    out=products[:, m], in0=acc[:].unsqueeze(1).to_broadcast([P, 2, D]), in1=d_tables[t][:], op=MULT
                )
                if last and m == 0:
                    nc.gpsimd.tensor_tensor(out=straight[:, 0], in0=straight[:, 0], in1=crossed[:, 0], op=ADD)
            if last:
                nc.vector.tensor_tensor(out=straight[:, 1], in0=straight[:, 1], in1=crossed[:, 1], op=ADD)
            else:
                nc.gpsimd.tensor_tensor(out=straight, in0=straight, in1=crossed, op=ADD)
            for m in range(2):
                stores.append((m, b, t, products))

        prepare = [(0, "w", (0, 1)), (0, "w", (1, 0)), (0, "w", (1, 1))]
        for members in x_sets[1:]:
            for t in members:
                prepare += [(first_use[members[0]] - 3, "x", (t, half)) for half in range(2)]
            for t in members:
                if t in T_POSITIONS:
                    prepare.append((first_use[t] - 2, "table", (t,)))
        sums = []
        stores = []

        def store_waiting(n):
            while len(stores) > n:
                m, b, t, products = stores[0]
                stores.remove(stores[0])
                nc.sync.dma_start(out=outs[m][:, b, t, :], in_=products[:, m, 0, :])

        state = {"prepared": 0, "summed": 0}
        to_quantise = []

        def prepare_piece(what, which, copy):
            if what == "w":
                turn_w(*which, copy)
                to_quantise.append((quantise_w, which))
            elif what == "table":
                turn_tables(*which)
            else:
                t, half = which
                if half == 0:
                    sort_tables(t)
                else:
                    for members in x_sets:
                        if t == members[-1]:
                            to_quantise.append((quantise_x, (members,)))
                turn_x(t, half, copy)

        def quantise_waiting():
            for call, which in to_quantise:
                call(*which)
            to_quantise.clear()

        def next_prepare():
            due, what, which = prepare[state["prepared"]]
            state["prepared"] += 1
            prepare_piece(what, which, nc.scalar.copy)

        def next_sum():
            arguments = sums[state["summed"]][1]
            state["summed"] += 1
            t_sums(*arguments)

        def matmuls(g):
            kind, n, unit = groups[g]
            return t_matmuls(*unit) if kind == "T" else d_matmuls(*unit)

        t = T_POSITIONS[0]
        prepare_piece("w", (0, 0), nc.vector.tensor_copy)
        prepare_piece("x", (t, 0), nc.scalar.copy)
        quantise_waiting()
        prepare_piece("x", (t, 1), nc.vector.tensor_copy)
        quantise_waiting()
        prepare_piece("table", (t,), nc.scalar.copy)
        next_prepare()
        quantise_waiting()
        accs = matmuls(0)
        summed = None
        for g, (kind, n, unit) in enumerate(groups):
            if kind == "T":
                t, m, pair = unit
                products = t_products(t, pair, accs, GPSIMD_BLOCKS[n % len(GPSIMD_BLOCKS)])
                if pair == 0:
                    summed = work.tile([P, B, 2, 2, P], F32, tag="t_summed", bufs=2)
                for b in range(0, B, 2):
                    sums.append((g + LAG, (t, m, pair, b, products, summed)))
            else:
                d_products(*unit, accs, g + 1 == len(groups))
            if g < 6 or (g - 4) % 7 == 6:
                quantise_waiting()
            if g + 1 < len(groups):
                accs = matmuls(g + 1)
            count = 0
            while state["prepared"] < len(prepare) and count < CHUNKS[kind] and prepare[state["prepared"]][0] <= g + AHEAD * (count == 0):
                next_prepare()
                count += 1
            while count < CHUNKS[kind] and state["summed"] < len(sums) and sums[state["summed"]][0] <= g:
                next_sum()
                count += 1
            store_waiting(2 * 0 if g + 1 < len(groups) else 0)
        while state["summed"] < len(sums):
            next_sum()
